import numpy as np
import ml_dtypes


def mxq(x, axis, fmt="e4m3"):
    dtype, down = {"e4m3": (ml_dtypes.float8_e4m3fn, 7), "e5m2": (ml_dtypes.float8_e5m2, 14)}[fmt]
    v = np.moveaxis(np.asarray(x, np.float32).astype(ml_dtypes.bfloat16).astype(np.float64), axis, -1)
    blocks = v.reshape(v.shape[:-1] + (-1, 32))
    amax = np.abs(blocks).max(-1, keepdims=True)
    byte = np.maximum(np.where(amax > 0, np.frexp(amax)[1] - 1 + 127, 0) - down, 1)
    scale = np.exp2(byte - 127.0)
    codes = (blocks / scale).astype(np.float32).astype(dtype).astype(np.float64)
    return np.moveaxis((codes * scale).reshape(v.shape), -1, axis)


WIDE = False


def mx_kscale(k):
    if not WIDE:
        return np.ones(k)
    levels = np.array([10, -10, 5, -5, 0])
    a = np.random.permutation(np.resize(levels, k // 512 * 4)).reshape(k // 512, 4)
    idx = np.arange(k)
    return np.exp2(a[idx // 512, idx % 128 // 32])


BF16 = ml_dtypes.bfloat16


def bf(x):
    return np.asarray(x, np.float32).astype(BF16)


def f64(x):
    return np.asarray(x).astype(np.float64)


B, S, C = 8, 512, 1024


def setup_inputs():
    a = np.log(mx_kscale(S))
    return {"k": bf(np.random.standard_normal((B, S, C)) - a[None, :, None]),
            "v": bf(np.random.standard_normal((B, S, C)) * 2.0),
            "bias_position": bf(np.random.standard_normal((S, S)) * 1.5 + a[None, :])}


def reference(k, v, bias_position):
    ek = np.exp(f64(k))
    eb = np.exp(f64(bias_position))
    ebq = mxq(eb, 1, "e4m3")
    numerator = ebq @ mxq(ek * f64(v), 1, "e4m3")
    denominator = ebq @ mxq(ek, 1, "e4m3")
    return numerator / denominator

@@ -1,0 +1,175 @@
+from contextlib import ExitStack
+
+import concourse.mybir as mybir
+from concourse.masks import make_identity
+
+BF16 = mybir.dt.bfloat16
+F32 = mybir.dt.float32
+U32 = mybir.dt.uint32
+U8 = mybir.dt.uint8
+FP8X4 = mybir.dt.float8_e4m3fn_x4
+ACT = mybir.ActivationFunctionType
+MULT = mybir.AluOpType.mult
+
+B, S, C = 8, 512, 1024
+P = 128
+PACK = 4
+COLS = 512
+UNITS = B * (C // COLS)
+T_TILES = S // P
+
+EXP_LEAD = 9
+EARLY_UNITS = 9
+
+FLOPS = 2 * 2 * B * S * S * C
+
+
+def tile_freetransatt_pa_t_kernel(tc, k, v, bias_position, out):
+    nc = tc.nc
+    with ExitStack() as ctx:
+        ctx.enter_context(tc.manual_schedule())
+        const = ctx.enter_context(tc.tile_pool(name="const", bufs=1))
+        v_pool = ctx.enter_context(tc.tile_pool(name="v", bufs=4))
+        ek_pool = ctx.enter_context(tc.tile_pool(name="ek", bufs=EXP_LEAD))
+        bf_pool = ctx.enter_context(tc.tile_pool(name="bf", bufs=2))
+        code_pool = ctx.enter_context(tc.tile_pool(name="codes", bufs=EARLY_UNITS + 1))
+
+        eb_codes = const.tile([P, S], U32, align_bytes=64)
+        eb_scales = const.tile([P, S], U8, align_bytes=64)
+        k_sb = []
+        v_sb = []
+        ek_f32 = {}
+        codes = {}
+        rec = {}
+
+        def unit_slices(u):
+            b, h = divmod(u, C // COLS)
+            return b, slice(h * COLS, (h + 1) * COLS)
+
+        def exponential(u):
+            b, cols = unit_slices(u)
+            ek = ek_pool.tile([P, COLS, PACK], F32)
+            nc.scalar.activation(
+                out=ek[:], in_=k_sb[b][:, :, cols].rearrange("p j c -> p c j"), func=ACT.Exp
+            )
+            ek_f32[u] = ek
+
+        def quantise(u):
+            b, cols = unit_slices(u)
+            ek = ek_f32[u]
+            ek_bf = bf_pool.tile([P, COLS, PACK], BF16, align_bytes=64)
+            nc.vector.tensor_copy(out=ek_bf[:], in_=ek[:])
+            ekv_bf = bf_pool.tile([P, COLS, PACK], BF16, align_bytes=64)
+            nc.vector.tensor_tensor(
+                out=ekv_bf[:],
+                in0=ek[:],
+                in1=v_sb[b][:, :, cols].rearrange("p j c -> p c j"),
+                op=MULT,
+            )
+            ek_codes = code_pool.tile([P, COLS], U32, align_bytes=64)
+            ek_scales = code_pool.tile([P, COLS], U8, align_bytes=64)
+            nc.vector.quantize_mx(
+                out=ek_codes[:].bitcast(FP8X4),
+                scales=ek_scales[:],
+                in_=ek_bf[:].rearrange("p c j -> p (c j)"),
+            )
+            ekv_codes = code_pool.tile([P, COLS], U32, align_bytes=64)
+            ekv_scales = code_pool.tile([P, COLS], U8, align_bytes=64)
+            nc.vector.quantize_mx(
+                out=ekv_codes[:].bitcast(FP8X4),
+                scales=ekv_scales[:],
+                in_=ekv_bf[:].rearrange("p c j -> p (c j)"),
+            )
+            codes[u] = (ek_codes, ek_scales, ekv_codes, ekv_scales)
+
+        with tc.tile_pool(name="k", bufs=3) as k_pool:
+            with tc.tile_pool(name="setup", bufs=1) as setup:
+                bias_sb = setup.tile([P, T_TILES, S], BF16)
+                nc.sync.dma_start(
+                    out=bias_sb[:], in_=bias_position.rearrange("(a p) s -> p a s", p=P)
+                )
+                for b in range(B):
+                    k_b = k_pool.tile([P, PACK, C], BF16)
+                    nc.sync.dma_start(out=k_b[:], in_=k[b].rearrange("(p j) c -> p j c", j=PACK))
+                    k_sb.append(k_b)
+                    v_b = v_pool.tile([P, PACK, C], BF16)
+                    nc.sync.dma_start(out=v_b[:], in_=v[b].rearrange("(p j) c -> p j c", j=PACK))
+                    v_sb.append(v_b)
+
+                ident = setup.tile([P, P], BF16)
+                make_identity(nc, ident[:])
+                eb_rows = setup.tile([P, T_TILES, PACK, P], BF16)
+                eb_bf = setup.tile([P, S, PACK], BF16, align_bytes=64)
+                with tc.psum_pool(name="tp", bufs=2) as tp_pool:
+                    for a in range(T_TILES):
+                        nc.scalar.activation(
+                            out=eb_rows[:, a],
+                            in_=bias_sb[:, a, :].rearrange("p (q j) -> p j q", j=PACK),
+                            func=ACT.Exp,
+                        )
+                        eb_t = tp_pool.tile([P, PACK, P], BF16)
+                        for j in range(PACK):
+                            nc.tensor.transpose(eb_t[:, j, :], eb_rows[:, a, j, :], ident[:])
+                        nc.vector.tensor_copy(
+                            out=eb_bf[:, a * P : (a + 1) * P, :],
+                            in_=eb_t[:].rearrange("q j t -> q t j"),
+                        )
+                nc.vector.quantize_mx(
+                    out=eb_codes[:].bitcast(FP8X4),
+                    scales=eb_scales[:],
+                    in_=eb_bf[:].rearrange("q t j -> q (t j)"),
+                )
+
+            for u in range(EXP_LEAD):
+                exponential(u)
+            for u in range(EARLY_UNITS):
+                quantise(u)
+                if u + EXP_LEAD < UNITS:
+                    exponential(u + EXP_LEAD)
+
+        rec_pool = ctx.enter_context(tc.tile_pool(name="rec", bufs=3))
+        out_pool = ctx.enter_context(tc.tile_pool(name="out", bufs=2 * T_TILES))
+        den_pool = ctx.enter_context(tc.psum_pool(name="den", bufs=T_TILES))
+        num_pool = ctx.enter_context(tc.psum_pool(name="num", bufs=T_TILES))
+
+        def mx_pass(acc, a, rhs_codes, rhs_scales):
+            t_cols = slice(a * P, (a + 1) * P)
+            nc.tensor.matmul_mx(
+                out=acc[:],
+                lhsT=eb_codes[:, t_cols].bitcast(FP8X4),
+                lhsT_scale=eb_scales[:, t_cols],
+                rhs=rhs_codes[:].bitcast(FP8X4),
+                rhs_scale=rhs_scales[:],
+                start=True,
+                stop=True,
+            )
+
+        def reciprocal(u):
+            ek_codes, ek_scales = codes[u][0], codes[u][1]
+            rec_u = rec_pool.tile([P, T_TILES, COLS], F32)
+            for a in range(T_TILES):
+                den = den_pool.tile([P, COLS], F32)
+                mx_pass(den, a, ek_codes, ek_scales)
+                nc.scalar.activation(out=rec_u[:, a, :], in_=den[:], func=ACT.Abs_reciprocal_sqrt)
+            for a in range(T_TILES):
+                nc.scalar.activation(out=rec_u[:, a, :], in_=rec_u[:, a, :], func=ACT.Square)
+            rec[u] = rec_u
+
+        def divide(u):
+            b, cols = unit_slices(u)
+            ekv_codes, ekv_scales = codes[u][2], codes[u][3]
+            for a in range(T_TILES):
+                num = num_pool.tile([P, COLS], F32)
+                mx_pass(num, a, ekv_codes, ekv_scales)
+                res = out_pool.tile([P, COLS], F32)
+                nc.vector.tensor_tensor(out=res[:], in0=num[:], in1=rec[u][:, a, :], op=MULT)
+                nc.sync.dma_start(out=out[b, a * P : (a + 1) * P, cols], in_=res[:])
+
+        for r in range(UNITS + 1):
+            if r < UNITS:
+                reciprocal(r)
+            if r >= 1:
+                divide(r - 1)
+            late = EARLY_UNITS + r // 2
+            if r % 2 == 1 and late < UNITS:
+                quantise(late)

@@ -151,8 +151,10 @@ def tile_freetransatt_pa_t_kernel(tc, k, v, bias_position, out):
                 den = den_pool.tile([P, COLS], F32)
                 mx_pass(den, a, ek_codes, ek_scales)
                 nc.scalar.activation(out=rec_u[:, a, :], in_=den[:], func=ACT.Abs_reciprocal_sqrt)
-            for a in range(T_TILES):
+            for a in range(T_TILES - 1):
                 nc.scalar.activation(out=rec_u[:, a, :], in_=rec_u[:, a, :], func=ACT.Square)
+            last = rec_u[:, T_TILES - 1, :]
+            nc.gpsimd.tensor_tensor(out=last, in0=last, in1=last, op=MULT)
             rec[u] = rec_u
 
         def divide(u):

@@ -39,6 +39,7 @@ def tile_freetransatt_pa_t_kernel(tc, k, v, bias_position, out):
         k_sb = []
         v_sb = []
         ek_f32 = {}
+        ekv_bf16 = {}
         codes = {}
         rec = {}
 
@@ -54,17 +55,26 @@ def tile_freetransatt_pa_t_kernel(tc, k, v, bias_position, out):
             )
             ek_f32[u] = ek
 
-        def quantise(u):
+        def multiply_by_v(u, engine):
             b, cols = unit_slices(u)
-            ek = ek_f32[u]
-            ek_bf = bf_pool.tile([P, COLS, PACK], BF16, align_bytes=64)
-            nc.vector.tensor_copy(out=ek_bf[:], in_=ek[:])
             ekv_bf = bf_pool.tile([P, COLS, PACK], BF16, align_bytes=64)
-            nc.vector.tensor_tensor(
+            engine.tensor_tensor(
                 out=ekv_bf[:],
-                in0=ek[:],
+                in0=ek_f32[u][:],
                 in1=v_sb[b][:, :, cols].rearrange("p j c -> p c j"),
                 op=MULT,
+            )
+            ekv_bf16[u] = ekv_bf
+
+        def quantise(u):
+            ek_bf = bf_pool.tile([P, COLS, PACK], BF16, align_bytes=64)
+            nc.vector.tensor_copy(out=ek_bf[:], in_=ek_f32[u][:])
+            ekv_codes = code_pool.tile([P, COLS], U32, align_bytes=64)
+            ekv_scales = code_pool.tile([P, COLS], U8, align_bytes=64)
+            nc.vector.quantize_mx(
+                out=ekv_codes[:].bitcast(FP8X4),
+                scales=ekv_scales[:],
+                in_=ekv_bf16[u][:].rearrange("p c j -> p (c j)"),
             )
             ek_codes = code_pool.tile([P, COLS], U32, align_bytes=64)
             ek_scales = code_pool.tile([P, COLS], U8, align_bytes=64)
@@ -72,13 +82,6 @@ def tile_freetransatt_pa_t_kernel(tc, k, v, bias_position, out):
                 out=ek_codes[:].bitcast(FP8X4),
                 scales=ek_scales[:],
                 in_=ek_bf[:].rearrange("p c j -> p (c j)"),
-            )
-            ekv_codes = code_pool.tile([P, COLS], U32, align_bytes=64)
-            ekv_scales = code_pool.tile([P, COLS], U8, align_bytes=64)
-            nc.vector.quantize_mx(
-                out=ekv_codes[:].bitcast(FP8X4),
-                scales=ekv_scales[:],
-                in_=ekv_bf[:].rearrange("p c j -> p (c j)"),
             )
             codes[u] = (ek_codes, ek_scales, ekv_codes, ekv_scales)
 
@@ -123,6 +126,7 @@ def tile_freetransatt_pa_t_kernel(tc, k, v, bias_position, out):
             for u in range(EXP_LEAD):
                 exponential(u)
             for u in range(EARLY_UNITS):
+                multiply_by_v(u, nc.vector)
                 quantise(u)
                 if u + EXP_LEAD < UNITS:
                     exponential(u + EXP_LEAD)
@@ -151,10 +155,8 @@ def tile_freetransatt_pa_t_kernel(tc, k, v, bias_position, out):
                 den = den_pool.tile([P, COLS], F32)
                 mx_pass(den, a, ek_codes, ek_scales)
                 nc.scalar.activation(out=rec_u[:, a, :], in_=den[:], func=ACT.Abs_reciprocal_sqrt)
-            for a in range(T_TILES - 1):
+            for a in range(T_TILES):
                 nc.scalar.activation(out=rec_u[:, a, :], in_=rec_u[:, a, :], func=ACT.Square)
-            last = rec_u[:, T_TILES - 1, :]
-            nc.gpsimd.tensor_tensor(out=last, in0=last, in1=last, op=MULT)
             rec[u] = rec_u
 
         def divide(u):
@@ -167,6 +169,7 @@ def tile_freetransatt_pa_t_kernel(tc, k, v, bias_position, out):
                 nc.vector.tensor_tensor(out=res[:], in0=num[:], in1=rec[u][:, a, :], op=MULT)
                 nc.sync.dma_start(out=out[b, a * P : (a + 1) * P, cols], in_=res[:])
 
+        multiply_by_v(EARLY_UNITS, nc.gpsimd)
         for r in range(UNITS + 1):
             if r < UNITS:
                 reciprocal(r)
@@ -174,4 +177,6 @@ def tile_freetransatt_pa_t_kernel(tc, k, v, bias_position, out):
                 divide(r - 1)
             late = EARLY_UNITS + r // 2
             if r % 2 == 1 and late < UNITS:
+                if late + 1 < UNITS:
+                    multiply_by_v(late + 1, nc.gpsimd)
                 quantise(late)

@@ -18,7 +18,7 @@ COLS = 512
 UNITS = B * (C // COLS)
 T_TILES = S // P
 
-EXP_LEAD = 9
+EXP_LEAD = 11
 EARLY_UNITS = 9
 
 FLOPS = 2 * 2 * B * S * S * C
@@ -91,13 +91,22 @@ def tile_freetransatt_pa_t_kernel(tc, k, v, bias_position, out):
                 nc.sync.dma_start(
                     out=bias_sb[:], in_=bias_position.rearrange("(a p) s -> p a s", p=P)
                 )
+
+                def load_v():
+                    v_b = v_pool.tile([P, PACK, C], BF16)
+                    nc.sync.dma_start(
+                        out=v_b[:], in_=v[len(v_sb)].rearrange("(p j) c -> p j c", j=PACK)
+                    )
+                    v_sb.append(v_b)
+
                 for b in range(B):
                     k_b = k_pool.tile([P, PACK, C], BF16)
                     nc.sync.dma_start(out=k_b[:], in_=k[b].rearrange("(p j) c -> p j c", j=PACK))
                     k_sb.append(k_b)
-                    v_b = v_pool.tile([P, PACK, C], BF16)
-                    nc.sync.dma_start(out=v_b[:], in_=v[b].rearrange("(p j) c -> p j c", j=PACK))
-                    v_sb.append(v_b)
+                    if b % 2 == 0:
+                        load_v()
+                for b in range(B // 2, B):
+                    load_v()
 
                 ident = setup.tile([P, P], BF16)
                 make_identity(nc, ident[:])

@@ -20,6 +20,9 @@ T_TILES = S // P
 
 EXP_LEAD = 11
 EARLY_UNITS = 9
+SHARE = slice(0, COLS // 2)
+REST = slice(COLS // 2, COLS)
+WHOLE = slice(0, COLS)
 
 FLOPS = 2 * 2 * B * S * S * C
 
@@ -32,15 +35,18 @@ def tile_freetransatt_pa_t_kernel(tc, k, v, bias_position, out):
         v_pool = ctx.enter_context(tc.tile_pool(name="v", bufs=4))
         ek_pool = ctx.enter_context(tc.tile_pool(name="ek", bufs=EXP_LEAD))
         bf_pool = ctx.enter_context(tc.tile_pool(name="bf", bufs=2))
-        code_pool = ctx.enter_context(tc.tile_pool(name="codes", bufs=EARLY_UNITS + 1))
+        share_pool = ctx.enter_context(tc.tile_pool(name="share", bufs=1))
+        code_pool = ctx.enter_context(tc.tile_pool(name="codes", bufs=2 * (EARLY_UNITS + 1)))
 
         eb_codes = const.tile([P, S], U32, align_bytes=64)
         eb_scales = const.tile([P, S], U8, align_bytes=64)
         k_sb = []
         v_sb = []
         ek_f32 = {}
+        ek_bf16 = {}
         ekv_bf16 = {}
-        codes = {}
+        ek_codes = {}
+        ekv_codes = {}
         rec = {}
 
         def unit_slices(u):
@@ -55,42 +61,63 @@ def tile_freetransatt_pa_t_kernel(tc, k, v, bias_position, out):
             )
             ek_f32[u] = ek
 
-        def multiply_by_v(u, engine):
+        def multiply_by_v(u, engine, part):
             b, cols = unit_slices(u)
-            ekv_bf = bf_pool.tile([P, COLS, PACK], BF16, align_bytes=64)
+            width = part.stop - part.start
+            if part == SHARE:
+                ekv_share = share_pool.tile([P, width, PACK], BF16, align_bytes=64)
+                ekv_bf = ekv_share
+            elif part == REST:
+                ekv_rest = bf_pool.tile([P, width, PACK], BF16, align_bytes=64)
+                ekv_bf = ekv_rest
+            else:
+                ekv_whole = bf_pool.tile([P, width, PACK], BF16, align_bytes=64)
+                ekv_bf = ekv_whole
             engine.tensor_tensor(
                 out=ekv_bf[:],
-                in0=ek_f32[u][:],
-                in1=v_sb[b][:, :, cols].rearrange("p j c -> p c j"),
+                in0=ek_f32[u][:, part, :],
+                in1=v_sb[b][:, :, cols.start + part.start : cols.start + part.stop].rearrange(
+                    "p j c -> p c j"
+                ),
                 op=MULT,
             )
-            ekv_bf16[u] = ekv_bf
+            ekv_bf16[(u, part.start)] = ekv_bf
 
-        def quantise(u):
+        def round_ek(u):
             ek_bf = bf_pool.tile([P, COLS, PACK], BF16, align_bytes=64)
             nc.vector.tensor_copy(out=ek_bf[:], in_=ek_f32[u][:])
-            ekv_codes = code_pool.tile([P, COLS], U32, align_bytes=64)
-            ekv_scales = code_pool.tile([P, COLS], U8, align_bytes=64)
+            ek_bf16[u] = ek_bf
+
+        def new_codes():
+            unit_codes = code_pool.tile([P, COLS], U32, align_bytes=64)
+            unit_scales = code_pool.tile([P, COLS], U8, align_bytes=64)
+            return unit_codes, unit_scales
+
+        def quantise(values, codes, part):
             nc.vector.quantize_mx(
-                out=ekv_codes[:].bitcast(FP8X4),
-                scales=ekv_scales[:],
-                in_=ekv_bf16[u][:].rearrange("p c j -> p (c j)"),
+                out=codes[0][:, part].bitcast(FP8X4),
+                scales=codes[1][:, part],
+                in_=values[:].rearrange("p c j -> p (c j)"),
             )
-            ek_codes = code_pool.tile([P, COLS], U32, align_bytes=64)
-            ek_scales = code_pool.tile([P, COLS], U8, align_bytes=64)
-            nc.vector.quantize_mx(
-                out=ek_codes[:].bitcast(FP8X4),
-                scales=ek_scales[:],
-                in_=ek_bf[:].rearrange("p c j -> p (c j)"),
-            )
-            codes[u] = (ek_codes, ek_scales, ekv_codes, ekv_scales)
+
+        def finish_late(u):
+            if u + 1 < UNITS:
+                multiply_by_v(u + 1, nc.vector, REST)
+            ek_codes[u] = new_codes()
+            quantise(ek_bf16[u], ek_codes[u], WHOLE)
+            if u + 1 < UNITS:
+                round_ek(u + 1)
+            ekv_codes[u] = new_codes()
+            quantise(ekv_bf16[(u, REST.start)], ekv_codes[u], REST)
+            quantise(ekv_bf16[(u, SHARE.start)], ekv_codes[u], SHARE)
+            if u + 1 < UNITS:
+                multiply_by_v(u + 1, nc.gpsimd, SHARE)
 
         with tc.tile_pool(name="k", bufs=3) as k_pool:
             with tc.tile_pool(name="setup", bufs=1) as setup:
                 bias_sb = setup.tile([P, T_TILES, S], BF16)
-                nc.sync.dma_start(
-                    out=bias_sb[:], in_=bias_position.rearrange("(a p) s -> p a s", p=P)
-                )
+                for a in range(T_TILES):
+                    nc.sync.dma_start(out=bias_sb[:, a, :], in_=bias_position[a * P : (a + 1) * P, :])
 
                 def load_v():
                     v_b = v_pool.tile([P, PACK, C], BF16)
@@ -101,7 +128,12 @@ def tile_freetransatt_pa_t_kernel(tc, k, v, bias_position, out):
 
                 for b in range(B):
                     k_b = k_pool.tile([P, PACK, C], BF16)
-                    nc.sync.dma_start(out=k_b[:], in_=k[b].rearrange("(p j) c -> p j c", j=PACK))
+                    width = COLS if b == 0 else C
+                    for c0 in range(0, C, width):
+                        nc.sync.dma_start(
+                            out=k_b[:, :, c0 : c0 + width],
+                            in_=k[b, :, c0 : c0 + width].rearrange("(p j) c -> p j c", j=PACK),
+                        )
                     k_sb.append(k_b)
                     if b % 2 == 0:
                         load_v()
@@ -134,35 +166,42 @@ def tile_freetransatt_pa_t_kernel(tc, k, v, bias_position, out):
 
             for u in range(EXP_LEAD):
                 exponential(u)
-            for u in range(EARLY_UNITS):
-                multiply_by_v(u, nc.vector)
-                quantise(u)
+            round_ek(0)
+            for u in range(EARLY_UNITS - 1):
+                multiply_by_v(u, nc.vector, WHOLE)
+                ek_codes[u] = new_codes()
+                quantise(ek_bf16[u], ek_codes[u], WHOLE)
+                round_ek(u + 1)
+                ekv_codes[u] = new_codes()
+                quantise(ekv_bf16[(u, 0)], ekv_codes[u], WHOLE)
                 if u + EXP_LEAD < UNITS:
                     exponential(u + EXP_LEAD)
+            multiply_by_v(EARLY_UNITS - 1, nc.vector, SHARE)
+            multiply_by_v(EARLY_UNITS - 1, nc.vector, REST)
+            finish_late(EARLY_UNITS - 1)
 
         rec_pool = ctx.enter_context(tc.tile_pool(name="rec", bufs=3))
         out_pool = ctx.enter_context(tc.tile_pool(name="out", bufs=2 * T_TILES))
         den_pool = ctx.enter_context(tc.psum_pool(name="den", bufs=T_TILES))
         num_pool = ctx.enter_context(tc.psum_pool(name="num", bufs=T_TILES))
 
-        def mx_pass(acc, a, rhs_codes, rhs_scales):
+        def mx_pass(acc, a, rhs):
             t_cols = slice(a * P, (a + 1) * P)
             nc.tensor.matmul_mx(
                 out=acc[:],
                 lhsT=eb_codes[:, t_cols].bitcast(FP8X4),
                 lhsT_scale=eb_scales[:, t_cols],
-                rhs=rhs_codes[:].bitcast(FP8X4),
-                rhs_scale=rhs_scales[:],
+                rhs=rhs[0][:].bitcast(FP8X4),
+                rhs_scale=rhs[1][:],
                 start=True,
                 stop=True,
             )
 
         def reciprocal(u):
-            ek_codes, ek_scales = codes[u][0], codes[u][1]
             rec_u = rec_pool.tile([P, T_TILES, COLS], F32)
             for a in range(T_TILES):
                 den = den_pool.tile([P, COLS], F32)
-                mx_pass(den, a, ek_codes, ek_scales)
+                mx_pass(den, a, ek_codes[u])
                 nc.scalar.activation(out=rec_u[:, a, :], in_=den[:], func=ACT.Abs_reciprocal_sqrt)
             for a in range(T_TILES):
                 nc.scalar.activation(out=rec_u[:, a, :], in_=rec_u[:, a, :], func=ACT.Square)
@@ -170,15 +209,13 @@ def tile_freetransatt_pa_t_kernel(tc, k, v, bias_position, out):
 
         def divide(u):
             b, cols = unit_slices(u)
-            ekv_codes, ekv_scales = codes[u][2], codes[u][3]
             for a in range(T_TILES):
                 num = num_pool.tile([P, COLS], F32)
-                mx_pass(num, a, ekv_codes, ekv_scales)
+                mx_pass(num, a, ekv_codes[u])
                 res = out_pool.tile([P, COLS], F32)
                 nc.vector.tensor_tensor(out=res[:], in0=num[:], in1=rec[u][:, a, :], op=MULT)
                 nc.sync.dma_start(out=out[b, a * P : (a + 1) * P, cols], in_=res[:])
 
-        multiply_by_v(EARLY_UNITS, nc.gpsimd)
         for r in range(UNITS + 1):
             if r < UNITS:
                 reciprocal(r)
@@ -186,6 +223,4 @@ def tile_freetransatt_pa_t_kernel(tc, k, v, bias_position, out):
                 divide(r - 1)
             late = EARLY_UNITS + r // 2
             if r % 2 == 1 and late < UNITS:
-                if late + 1 < UNITS:
-                    multiply_by_v(late + 1, nc.gpsimd)
-                quantise(late)
+                finish_late(late)

@@ -100,7 +100,7 @@ def tile_freetransatt_pa_t_kernel(tc, k, v, bias_position, out):
                 in_=values[:].rearrange("p c j -> p (c j)"),
             )
 
-        def finish_late(u):
+        def finish_late(u, square=None):
             if u + 1 < UNITS:
                 multiply_by_v(u + 1, nc.vector, REST)
             ek_codes[u] = new_codes()
@@ -109,6 +109,8 @@ def tile_freetransatt_pa_t_kernel(tc, k, v, bias_position, out):
                 round_ek(u + 1)
             ekv_codes[u] = new_codes()
             quantise(ekv_bf16[(u, REST.start)], ekv_codes[u], REST)
+            if square is not None:
+                nc.vector.tensor_tensor(out=square, in0=square, in1=square, op=MULT)
             quantise(ekv_bf16[(u, SHARE.start)], ekv_codes[u], SHARE)
             if u + 1 < UNITS:
                 multiply_by_v(u + 1, nc.gpsimd, SHARE)
@@ -197,13 +199,16 @@ def tile_freetransatt_pa_t_kernel(tc, k, v, bias_position, out):
                 stop=True,
             )
 
+        def finishes_late_before(r):
+            return r % 2 == 1 and EARLY_UNITS + r // 2 < UNITS
+
         def reciprocal(u):
             rec_u = rec_pool.tile([P, T_TILES, COLS], F32)
             for a in range(T_TILES):
                 den = den_pool.tile([P, COLS], F32)
                 mx_pass(den, a, ek_codes[u])
                 nc.scalar.activation(out=rec_u[:, a, :], in_=den[:], func=ACT.Abs_reciprocal_sqrt)
-            for a in range(T_TILES):
+            for a in range(T_TILES - 1 if finishes_late_before(u) else T_TILES):
                 nc.scalar.activation(out=rec_u[:, a, :], in_=rec_u[:, a, :], func=ACT.Square)
             rec[u] = rec_u
 
@@ -221,6 +226,5 @@ def tile_freetransatt_pa_t_kernel(tc, k, v, bias_position, out):
                 reciprocal(r)
             if r >= 1:
                 divide(r - 1)
-            late = EARLY_UNITS + r // 2
-            if r % 2 == 1 and late < UNITS:
-                finish_late(late)
+            if finishes_late_before(r):
+                finish_late(EARLY_UNITS + r // 2, square=rec[r][:, T_TILES - 1, :])

from contextlib import ExitStack

import concourse.mybir as mybir
from concourse.masks import make_identity

BF16 = mybir.dt.bfloat16
F32 = mybir.dt.float32
U32 = mybir.dt.uint32
U8 = mybir.dt.uint8
FP8X4 = mybir.dt.float8_e4m3fn_x4
ACT = mybir.ActivationFunctionType
MULT = mybir.AluOpType.mult

B, S, C = 8, 512, 1024
P = 128
PACK = 4
COLS = 512
UNITS = B * (C // COLS)
T_TILES = S // P

EXP_LEAD = 11
EARLY_UNITS = 9
SHARE = slice(0, COLS // 2)
REST = slice(COLS // 2, COLS)
WHOLE = slice(0, COLS)

FLOPS = 2 * 2 * B * S * S * C


def tile_freetransatt_pa_t_kernel(tc, k, v, bias_position, out):
    nc = tc.nc
    with ExitStack() as ctx:
        ctx.enter_context(tc.manual_schedule())
        const = ctx.enter_context(tc.tile_pool(name="const", bufs=1))
        v_pool = ctx.enter_context(tc.tile_pool(name="v", bufs=4))
        ek_pool = ctx.enter_context(tc.tile_pool(name="ek", bufs=EXP_LEAD))
        bf_pool = ctx.enter_context(tc.tile_pool(name="bf", bufs=2))
        share_pool = ctx.enter_context(tc.tile_pool(name="share", bufs=1))
        code_pool = ctx.enter_context(tc.tile_pool(name="codes", bufs=2 * (EARLY_UNITS + 1)))

        eb_codes = const.tile([P, S], U32, align_bytes=64)
        eb_scales = const.tile([P, S], U8, align_bytes=64)
        k_sb = []
        v_sb = []
        ek_f32 = {}
        ek_bf16 = {}
        ekv_bf16 = {}
        ek_codes = {}
        ekv_codes = {}
        rec = {}

        def unit_slices(u):
            b, h = divmod(u, C // COLS)
            return b, slice(h * COLS, (h + 1) * COLS)

        def exponential(u):
            b, cols = unit_slices(u)
            ek = ek_pool.tile([P, COLS, PACK], F32)
            nc.scalar.activation(
                out=ek[:], in_=k_sb[b][:, :, cols].rearrange("p j c -> p c j"), func=ACT.Exp
            )
            ek_f32[u] = ek

        def multiply_by_v(u, engine, part):
            b, cols = unit_slices(u)
            width = part.stop - part.start
            if part == SHARE:
                ekv_share = share_pool.tile([P, width, PACK], BF16, align_bytes=64)
                ekv_bf = ekv_share
            elif part == REST:
                ekv_rest = bf_pool.tile([P, width, PACK], BF16, align_bytes=64)
                ekv_bf = ekv_rest
            else:
                ekv_whole = bf_pool.tile([P, width, PACK], BF16, align_bytes=64)
                ekv_bf = ekv_whole
            engine.tensor_tensor(
                out=ekv_bf[:],
                in0=ek_f32[u][:, part, :],
                in1=v_sb[b][:, :, cols.start + part.start : cols.start + part.stop].rearrange(
                    "p j c -> p c j"
                ),
                op=MULT,
            )
            ekv_bf16[(u, part.start)] = ekv_bf

        def round_ek(u):
            ek_bf = bf_pool.tile([P, COLS, PACK], BF16, align_bytes=64)
            nc.vector.tensor_copy(out=ek_bf[:], in_=ek_f32[u][:])
            ek_bf16[u] = ek_bf

        def new_codes():
            unit_codes = code_pool.tile([P, COLS], U32, align_bytes=64)
            unit_scales = code_pool.tile([P, COLS], U8, align_bytes=64)
            return unit_codes, unit_scales

        def quantise(values, codes, part):
            nc.vector.quantize_mx(
                out=codes[0][:, part].bitcast(FP8X4),
                scales=codes[1][:, part],
                in_=values[:].rearrange("p c j -> p (c j)"),
            )

        def finish_late(u, square=None):
            if u + 1 < UNITS:
                multiply_by_v(u + 1, nc.vector, REST)
            ek_codes[u] = new_codes()
            quantise(ek_bf16[u], ek_codes[u], WHOLE)
            if u + 1 < UNITS:
                round_ek(u + 1)
            ekv_codes[u] = new_codes()
            quantise(ekv_bf16[(u, REST.start)], ekv_codes[u], REST)
            if square is not None:
                nc.vector.tensor_tensor(out=square, in0=square, in1=square, op=MULT)
            quantise(ekv_bf16[(u, SHARE.start)], ekv_codes[u], SHARE)
            if u + 1 < UNITS:
                multiply_by_v(u + 1, nc.gpsimd, SHARE)

        with tc.tile_pool(name="k", bufs=3) as k_pool:
            with tc.tile_pool(name="setup", bufs=1) as setup:
                bias_sb = setup.tile([P, T_TILES, S], BF16)
                for a in range(T_TILES):
                    nc.sync.dma_start(out=bias_sb[:, a, :], in_=bias_position[a * P : (a + 1) * P, :])

                def load_v():
                    v_b = v_pool.tile([P, PACK, C], BF16)
                    nc.sync.dma_start(
                        out=v_b[:], in_=v[len(v_sb)].rearrange("(p j) c -> p j c", j=PACK)
                    )
                    v_sb.append(v_b)

                for b in range(B):
                    k_b = k_pool.tile([P, PACK, C], BF16)
                    width = COLS if b == 0 else C
                    for c0 in range(0, C, width):
                        nc.sync.dma_start(
                            out=k_b[:, :, c0 : c0 + width],
                            in_=k[b, :, c0 : c0 + width].rearrange("(p j) c -> p j c", j=PACK),
                        )
                    k_sb.append(k_b)
                    if b % 2 == 0:
                        load_v()
                for b in range(B // 2, B):
                    load_v()

                ident = setup.tile([P, P], BF16)
                make_identity(nc, ident[:])
                eb_rows = setup.tile([P, T_TILES, PACK, P], BF16)
                eb_bf = setup.tile([P, S, PACK], BF16, align_bytes=64)
                with tc.psum_pool(name="tp", bufs=2) as tp_pool:
                    for a in range(T_TILES):
                        nc.scalar.activation(
                            out=eb_rows[:, a],
                            in_=bias_sb[:, a, :].rearrange("p (q j) -> p j q", j=PACK),
                            func=ACT.Exp,
                        )
                        eb_t = tp_pool.tile([P, PACK, P], BF16)
                        for j in range(PACK):
                            nc.tensor.transpose(eb_t[:, j, :], eb_rows[:, a, j, :], ident[:])
                        nc.vector.tensor_copy(
                            out=eb_bf[:, a * P : (a + 1) * P, :],
                            in_=eb_t[:].rearrange("q j t -> q t j"),
                        )
                nc.vector.quantize_mx(
                    out=eb_codes[:].bitcast(FP8X4),
                    scales=eb_scales[:],
                    in_=eb_bf[:].rearrange("q t j -> q (t j)"),
                )

            for u in range(EXP_LEAD):
                exponential(u)
            round_ek(0)
            for u in range(EARLY_UNITS - 1):
                multiply_by_v(u, nc.vector, WHOLE)
                ek_codes[u] = new_codes()
                quantise(ek_bf16[u], ek_codes[u], WHOLE)
                round_ek(u + 1)
                ekv_codes[u] = new_codes()
                quantise(ekv_bf16[(u, 0)], ekv_codes[u], WHOLE)
                if u + EXP_LEAD < UNITS:
                    exponential(u + EXP_LEAD)
            multiply_by_v(EARLY_UNITS - 1, nc.vector, SHARE)
            multiply_by_v(EARLY_UNITS - 1, nc.vector, REST)
            finish_late(EARLY_UNITS - 1)

        rec_pool = ctx.enter_context(tc.tile_pool(name="rec", bufs=3))
        out_pool = ctx.enter_context(tc.tile_pool(name="out", bufs=2 * T_TILES))
        den_pool = ctx.enter_context(tc.psum_pool(name="den", bufs=T_TILES))
        num_pool = ctx.enter_context(tc.psum_pool(name="num", bufs=T_TILES))

        def mx_pass(acc, a, rhs):
            t_cols = slice(a * P, (a + 1) * P)
            nc.tensor.matmul_mx(
                out=acc[:],
                lhsT=eb_codes[:, t_cols].bitcast(FP8X4),
                lhsT_scale=eb_scales[:, t_cols],
                rhs=rhs[0][:].bitcast(FP8X4),
                rhs_scale=rhs[1][:],
                start=True,
                stop=True,
            )

        def finishes_late_before(r):
            return r % 2 == 1 and EARLY_UNITS + r // 2 < UNITS

        def reciprocal(u):
            rec_u = rec_pool.tile([P, T_TILES, COLS], F32)
            for a in range(T_TILES):
                den = den_pool.tile([P, COLS], F32)
                mx_pass(den, a, ek_codes[u])
                nc.scalar.activation(out=rec_u[:, a, :], in_=den[:], func=ACT.Abs_reciprocal_sqrt)
            for a in range(T_TILES - 1 if finishes_late_before(u) else T_TILES):
                nc.scalar.activation(out=rec_u[:, a, :], in_=rec_u[:, a, :], func=ACT.Square)
            rec[u] = rec_u

        def divide(u):
            b, cols = unit_slices(u)
            for a in range(T_TILES):
                num = num_pool.tile([P, COLS], F32)
                mx_pass(num, a, ekv_codes[u])
                res = out_pool.tile([P, COLS], F32)
                nc.vector.tensor_tensor(out=res[:], in0=num[:], in1=rec[u][:, a, :], op=MULT)
                nc.sync.dma_start(out=out[b, a * P : (a + 1) * P, cols], in_=res[:])

        for r in range(UNITS + 1):
            if r < UNITS:
                reciprocal(r)
            if r >= 1:
                divide(r - 1)
            if finishes_late_before(r):
                finish_late(EARLY_UNITS + r // 2, square=rec[r][:, T_TILES - 1, :])
